import numpy as np
import ml_dtypes


def mxq(x, axis, fmt="e4m3"):
    dtype, down = {"e4m3": (ml_dtypes.float8_e4m3fn, 7), "e5m2": (ml_dtypes.float8_e5m2, 14)}[fmt]
    v = np.moveaxis(np.asarray(x, np.float32).astype(ml_dtypes.bfloat16).astype(np.float64), axis, -1)
    blocks = v.reshape(v.shape[:-1] + (-1, 32))
    amax = np.abs(blocks).max(-1, keepdims=True)
    byte = np.maximum(np.where(amax > 0, np.frexp(amax)[1] - 1 + 127, 0) - down, 1)
    scale = np.exp2(byte - 127.0)
    codes = (blocks / scale).astype(np.float32).astype(dtype).astype(np.float64)
    return np.moveaxis((codes * scale).reshape(v.shape), -1, axis)


WIDE = False


def mx_kscale(k):
    if not WIDE:
        return np.ones(k)
    levels = np.array([10, -10, 5, -5, 0])
    if k % 512:
        return np.exp2(np.random.permutation(np.resize(levels, k // 32))).repeat(32)
    a = np.empty((k // 512, 16))
    for p in range(k // 512):
        a[p, :8] = np.random.permutation(np.resize(levels, 8))
        for g in range(8):
            far = levels[np.abs(levels - a[p, g]) >= 10]
            a[p, g + 8] = far[np.random.randint(len(far))]
    return np.exp2(a.ravel()).repeat(32)


BF16 = ml_dtypes.bfloat16


def bf(x):
    return np.asarray(x, np.float32).astype(BF16)


def f64(x):
    return np.asarray(x).astype(np.float64)


N, D, L = 1024, 1024, 4


def setup_inputs():
    s = mx_kscale(D)
    return {"x": bf(np.random.standard_normal((N, D)) * s),
            "W1": bf(np.random.standard_normal((D, D)) / np.sqrt(D) / s[None, :])}


def reference(x, W1):
    h = mxq(f64(x), 1, "e4m3") @ mxq(f64(W1), 1, "e4m3").T
    a = h * h.T
    sq = a * a
    return sq / np.sum(sq, axis=1, keepdims=True)

@@ -1,0 +1,170 @@
+from contextlib import ExitStack
+
+import concourse.mybir as mybir
+from concourse.masks import make_identity
+
+FP8X4 = mybir.dt.float8_e4m3fn_x4
+F32 = mybir.dt.float32
+BF16 = mybir.dt.bfloat16
+U32 = mybir.dt.uint32
+U8 = mybir.dt.uint8
+ALU = mybir.AluOpType
+ACT = mybir.ActivationFunctionType
+AX = mybir.AxisListType
+
+P = 128
+N = 1024
+D = 1024
+WORD = 4
+PASSES = D // (P * WORD)
+WORD_BLOCKS = D // 2 // P
+TILES = N // P
+HALF = TILES // 2
+BANK = HALF * P
+PARTS = 4
+FLOPS = 2 * N * N * D
+
+
+def tile_gcn_pa_kernel(tc, x, W1, out):
+    nc = tc.nc
+    with ExitStack() as ctx:
+        const = ctx.enter_context(tc.tile_pool(name="const", bufs=1))
+        raw = ctx.enter_context(tc.tile_pool(name="raw", bufs=1))
+        keep = ctx.enter_context(tc.tile_pool(name="keep", bufs=1))
+        grp = ctx.enter_context(tc.tile_pool(name="grp", bufs=4))
+        work = ctx.enter_context(tc.tile_pool(name="work", bufs=3))
+        rows = ctx.enter_context(tc.tile_pool(name="rows", bufs=4))
+        small = ctx.enter_context(tc.tile_pool(name="small", bufs=8))
+        psum = ctx.enter_context(tc.psum_pool(name="psum", bufs=8))
+
+        operands = {"x": x, "w1": W1}
+        loaded = {}
+        for t in range(TILES):
+            for name in ("x", "w1"):
+                row_tile = raw.tile([P, D], BF16, name="raw_%s_%d" % (name, t))
+                nc.sync.dma_start(out=row_tile[:], in_=operands[name][t * P:(t + 1) * P, :])
+                loaded[(name, t)] = row_tile
+
+        ident = const.tile([P, P], F32, name="ident")
+        make_identity(nc, ident[:])
+        row_sums = const.tile([P, TILES, PARTS], F32, name="row_sums")
+        nc.vector.memset(row_sums[:], 0.0)
+        parts_used = [0] * TILES
+        sq = keep.tile([P, TILES, N], F32, name="sq")
+        codes = {}
+        scales = {}
+        for name in ("x", "w1"):
+            codes[name] = keep.tile([P, PASSES, N], U32, name="codes_" + name, align_bytes=64)
+            scales[name] = keep.tile([P, PASSES, N], U8, name="scales_" + name, align_bytes=64)
+
+        zeros = const.tile([P, BANK], BF16, name="zeros")
+        nc.vector.memset(zeros[:], 0.0)
+        unread = psum.tile([P, BANK], F32, name="bank")
+        for n in range(4):
+            nc.tensor.matmul(out=unread[:], lhsT=zeros[:, :P], rhs=zeros[:], start=True, stop=True)
+
+        def keep_busy(t):
+            unread = psum.tile([P, BANK], F32, name="bank")
+            nc.tensor.matmul(out=unread[:], lhsT=loaded[("x", t)][:, :P], rhs=loaded[("w1", t)][:, :BANK],
+                             start=True, stop=True)
+
+        def next_part(s):
+            c = parts_used[s]
+            parts_used[s] = c + 1
+            return row_sums[:, s, c:c + 1]
+
+        def copy_out(engine, dst, src):
+            if engine == "v":
+                nc.vector.tensor_copy(out=dst, in_=src)
+            else:
+                nc.scalar.copy(out=dst, in_=src)
+
+        def turn(name, t, engine):
+            words = loaded[(name, t)][:].bitcast(F32)
+            turned = psum.tile([P, BANK], F32, name="bank")
+            for q in range(WORD_BLOCKS):
+                g, u = divmod(q, 2)
+                nc.tensor.transpose(turned[:, q * P:(q + 1) * P],
+                                    words[:, 2 * P * g + u:2 * P * (g + 1):2], ident[:])
+            grouped = grp.tile([P, PASSES * P * WORD], BF16, name="grouped", align_bytes=64)
+            copy_out(engine,
+                     grouped[:].bitcast(F32).rearrange("p (g r u) -> p g r u", g=PASSES, u=2),
+                     turned[:].rearrange("p (g u r) -> p g r u", g=PASSES, u=2))
+            return grouped
+
+        def quantise(name, t, grouped):
+            for g in range(PASSES):
+                nc.vector.quantize_mx(
+                    out=codes[name][:, g, t * P:(t + 1) * P].bitcast(FP8X4),
+                    scales=scales[name][:, g, t * P:(t + 1) * P],
+                    in_=grouped[:, g * P * WORD:(g + 1) * P * WORD],
+                )
+
+        def moving_cuts(j0, j1):
+            cuts = []
+            j = j0
+            while j < j1:
+                blocks = 4 if j1 - j >= 4 else (2 if j1 - j >= 2 else 1)
+                cuts.append((j, j + blocks))
+                j += blocks
+            return cuts
+
+        def product(stationary, moving, s, j0, j1):
+            bank = psum.tile([P, BANK], F32, name="bank")
+            for (lo, hi) in moving_cuts(j0, j1):
+                for g in range(PASSES):
+                    nc.tensor.matmul_mx(
+                        out=bank[:, (lo - j0) * P:(hi - j0) * P],
+                        lhsT=codes[stationary][:, g, s * P:(s + 1) * P].bitcast(FP8X4),
+                        lhsT_scale=scales[stationary][:, g, s * P:(s + 1) * P],
+                        rhs=codes[moving][:, g, lo * P:hi * P].bitcast(FP8X4),
+                        rhs_scale=scales[moving][:, g, lo * P:hi * P],
+                        start=(g == 0),
+                        stop=(g == PASSES - 1),
+                    )
+            return bank
+
+        def squares(s, j0, j1, engine):
+            cols = (j1 - j0) * P
+            h = product("x", "w1", s, j0, j1)
+            h_t = product("w1", "x", s, j0, j1)
+            h_sbuf = work.tile([P, BANK], F32, name="h_sbuf")
+            copy_out(engine, h_sbuf[:, :cols], h[:, :cols])
+            a = work.tile([P, BANK], F32, name="a")
+            nc.vector.tensor_tensor(out=a[:, :cols], in0=h_t[:, :cols], in1=h_sbuf[:, :cols], op=ALU.mult)
+            nc.scalar.activation(out=sq[:, s, j0 * P:j1 * P], in_=a[:, :cols], func=ACT.Square,
+                                 accum_out=next_part(s))
+
+        def mirror(s, j0, j1):
+            cols = (j1 - j0) * P
+            bank = psum.tile([P, BANK], F32, name="bank")
+            for j in range(j0, j1):
+                nc.tensor.transpose(bank[:, (j - j0) * P:(j - j0 + 1) * P], sq[:, j, s * P:(s + 1) * P], ident[:])
+            nc.scalar.activation(out=sq[:, s, j0 * P:j1 * P], in_=bank[:, :cols], func=ACT.Copy,
+                                 accum_out=next_part(s))
+
+        def finish(s):
+            total = small.tile([P, 1], F32, name="total")
+            nc.vector.tensor_reduce(out=total[:], in_=row_sums[:, s, :], axis=AX.X, op=ALU.add)
+            inverse = small.tile([P, 1], F32, name="inverse")
+            nc.vector.reciprocal(out=inverse[:], in_=total[:])
+            adj = rows.tile([P, N], F32, name="adj")
+            nc.vector.tensor_scalar(out=adj[:], in0=sq[:, s, :], scalar1=inverse[:, 0:1], scalar2=None,
+                                    op0=ALU.mult)
+            nc.sync.dma_start(out=out[s * P:(s + 1) * P, :], in_=adj[:])
+
+        for t in range(TILES):
+            grouped_x = turn("x", t, "s")
+            grouped_w1 = turn("w1", t, "v" if t % 2 == 0 else "s")
+            keep_busy(t)
+            quantise("x", t, grouped_x)
+            quantise("w1", t, grouped_w1)
+        for s in range(TILES):
+            if s < HALF:
+                squares(s, s, HALF, "v")
+            squares(s, max(s, HALF), TILES, "s" if s % 2 == 0 else "v")
+            if s > 0:
+                mirror(s, 0, min(s, HALF))
+            if s > HALF:
+                mirror(s, HALF, s)
+            finish(s)

@@ -31,11 +31,12 @@ def tile_gcn_pa_kernel(tc, x, W1, out):
         const = ctx.enter_context(tc.tile_pool(name="const", bufs=1))
         raw = ctx.enter_context(tc.tile_pool(name="raw", bufs=1))
         keep = ctx.enter_context(tc.tile_pool(name="keep", bufs=1))
-        grp = ctx.enter_context(tc.tile_pool(name="grp", bufs=4))
-        work = ctx.enter_context(tc.tile_pool(name="work", bufs=3))
+        grp = ctx.enter_context(tc.tile_pool(name="grp", bufs=6))
+        work = ctx.enter_context(tc.tile_pool(name="work", bufs=4))
         rows = ctx.enter_context(tc.tile_pool(name="rows", bufs=4))
         small = ctx.enter_context(tc.tile_pool(name="small", bufs=8))
         psum = ctx.enter_context(tc.psum_pool(name="psum", bufs=8))
+        ctx.enter_context(tc.manual_schedule())
 
         operands = {"x": x, "w1": W1}
         loaded = {}
@@ -47,6 +48,8 @@ def tile_gcn_pa_kernel(tc, x, W1, out):
 
         ident = const.tile([P, P], F32, name="ident")
         make_identity(nc, ident[:])
+        zeros = const.tile([P, BANK], BF16, name="zeros")
+        nc.vector.memset(zeros[:], 0.0)
         row_sums = const.tile([P, TILES, PARTS], F32, name="row_sums")
         nc.vector.memset(row_sums[:], 0.0)
         parts_used = [0] * TILES
@@ -57,8 +60,6 @@ def tile_gcn_pa_kernel(tc, x, W1, out):
             codes[name] = keep.tile([P, PASSES, N], U32, name="codes_" + name, align_bytes=64)
             scales[name] = keep.tile([P, PASSES, N], U8, name="scales_" + name, align_bytes=64)
 
-        zeros = const.tile([P, BANK], BF16, name="zeros")
-        nc.vector.memset(zeros[:], 0.0)
         unread = psum.tile([P, BANK], F32, name="bank")
         for n in range(4):
             nc.tensor.matmul(out=unread[:], lhsT=zeros[:, :P], rhs=zeros[:], start=True, stop=True)
@@ -79,13 +80,29 @@ def tile_gcn_pa_kernel(tc, x, W1, out):
             else:
                 nc.scalar.copy(out=dst, in_=src)
 
-        def turn(name, t, engine):
+        def split_words(engine, name, t):
+            split = grp.tile([P, BANK], F32, name="split")
+            dst = split[:].rearrange("p (g u i) -> p g u i", g=PASSES, u=2)
+            src = loaded[(name, t)][:].bitcast(F32).rearrange("p (g i u) -> p g u i", g=PASSES, u=2)
+            if engine == "v":
+                nc.vector.tensor_copy(out=dst, in_=src)
+            elif engine == "s":
+                nc.scalar.copy(out=dst, in_=src)
+            else:
+                nc.gpsimd.tensor_copy(out=dst, in_=src)
+            return split
+
+        def turn(name, t, split=None):
             words = loaded[(name, t)][:].bitcast(F32)
             turned = psum.tile([P, BANK], F32, name="bank")
             for q in range(WORD_BLOCKS):
                 g, u = divmod(q, 2)
-                nc.tensor.transpose(turned[:, q * P:(q + 1) * P],
-                                    words[:, 2 * P * g + u:2 * P * (g + 1):2], ident[:])
+                block = (words[:, 2 * P * g + u:2 * P * (g + 1):2] if split is None
+                         else split[:, q * P:(q + 1) * P])
+                nc.tensor.transpose(turned[:, q * P:(q + 1) * P], block, ident[:])
+            return turned
+
+        def group(engine, turned):
             grouped = grp.tile([P, PASSES * P * WORD], BF16, name="grouped", align_bytes=64)
             copy_out(engine,
                      grouped[:].bitcast(F32).rearrange("p (g r u) -> p g r u", g=PASSES, u=2),
@@ -124,47 +141,153 @@ def tile_gcn_pa_kernel(tc, x, W1, out):
                     )
             return bank
 
-        def squares(s, j0, j1, engine):
-            cols = (j1 - j0) * P
+        class_of = {}
+
+        def products(s, j0, j1):
             h = product("x", "w1", s, j0, j1)
             h_t = product("w1", "x", s, j0, j1)
+            return [s, j0, j1, h, h_t]
+
+        def copy_h(p, engine):
+            s, j0, j1, h, h_t = p
+            cols = (j1 - j0) * P
             h_sbuf = work.tile([P, BANK], F32, name="h_sbuf")
             copy_out(engine, h_sbuf[:, :cols], h[:, :cols])
             a = work.tile([P, BANK], F32, name="a")
-            nc.vector.tensor_tensor(out=a[:, :cols], in0=h_t[:, :cols], in1=h_sbuf[:, :cols], op=ALU.mult)
+            p.extend([h_sbuf, a])
+
+        def multiply(p, part=0, parts=1):
+            s, j0, j1, h, h_t, h_sbuf, a = p
+            cols = (j1 - j0) * P
+            lo, hi = part * cols // parts, (part + 1) * cols // parts
+            nc.vector.tensor_tensor(out=a[:, lo:hi], in0=h_t[:, lo:hi], in1=h_sbuf[:, lo:hi], op=ALU.mult)
+
+        def square(p):
+            s, j0, j1, h, h_t, h_sbuf, a = p
+            cols = (j1 - j0) * P
             nc.scalar.activation(out=sq[:, s, j0 * P:j1 * P], in_=a[:, :cols], func=ACT.Square,
                                  accum_out=next_part(s))
 
-        def mirror(s, j0, j1):
-            cols = (j1 - j0) * P
+        def mirror_turn(s, j0, j1):
             bank = psum.tile([P, BANK], F32, name="bank")
             for j in range(j0, j1):
                 nc.tensor.transpose(bank[:, (j - j0) * P:(j - j0 + 1) * P], sq[:, j, s * P:(s + 1) * P], ident[:])
-            nc.scalar.activation(out=sq[:, s, j0 * P:j1 * P], in_=bank[:, :cols], func=ACT.Copy,
+            return bank
+
+        def mirror_copy(s, j0, j1, bank, engine="s"):
+            if engine == "v":
+                nc.vector.tensor_scalar(out=sq[:, s, j0 * P:j1 * P], in0=bank[:, :(j1 - j0) * P], scalar1=1.0,
+                                        scalar2=0.0, op0=ALU.mult, op1=ALU.add, accum_out=next_part(s))
+                return
+            nc.scalar.activation(out=sq[:, s, j0 * P:j1 * P], in_=bank[:, :(j1 - j0) * P], func=ACT.Copy,
                                  accum_out=next_part(s))
 
-        def finish(s):
-            total = small.tile([P, 1], F32, name="total")
-            nc.vector.tensor_reduce(out=total[:], in_=row_sums[:, s, :], axis=AX.X, op=ALU.add)
-            inverse = small.tile([P, 1], F32, name="inverse")
-            nc.vector.reciprocal(out=inverse[:], in_=total[:])
-            adj = rows.tile([P, N], F32, name="adj")
-            nc.vector.tensor_scalar(out=adj[:], in0=sq[:, s, :], scalar1=inverse[:, 0:1], scalar2=None,
-                                    op0=ALU.mult)
-            nc.sync.dma_start(out=out[s * P:(s + 1) * P, :], in_=adj[:])
+        totals = {}
 
+        def total(s):
+            t = small.tile([P, 1], F32, name="total")
+            nc.vector.tensor_reduce(out=t[:], in_=row_sums[:, s, :], axis=AX.X, op=ALU.add)
+            totals[s] = t
+
+        def invert(s):
+            inverse = small.tile([P, 1], F32, name="inverse")
+            nc.vector.reciprocal(out=inverse[:], in_=totals[s][:])
+            totals[s] = inverse
+
+        adjs = {}
+
+        def divide_part(s, i, e):
+            if e == "-":
+                return
+            if s not in adjs:
+                adjs[s] = rows.tile([P, N], F32, name="adj")
+            adj = adjs[s]
+            c = slice(i * N // 2, (i + 1) * N // 2)
+            if e in "VG":
+                c = slice(0, N)
+            if e in "vV":
+                nc.vector.tensor_scalar(out=adj[:, c], in0=sq[:, s, c], scalar1=totals[s][:, 0:1], scalar2=None,
+                                        op0=ALU.mult)
+            elif e in "gG":
+                nc.gpsimd.tensor_scalar(out=adj[:, c], in0=sq[:, s, c], scalar1=totals[s][:, 0:1], scalar2=0.0,
+                                        op0=ALU.mult, op1=ALU.add)
+            else:
+                nc.scalar.activation(out=adj[:, c], in_=sq[:, s, c], func=ACT.Copy, scale=totals[s][:, 0:1])
+            nc.sync.dma_start(out=out[s * P:(s + 1) * P, c], in_=adj[:, c])
+
+        DIV = ["vv","vv","vv","vv","vv","vv","vv","vs"]
+        early = {}
+        splits = {}
         for t in range(TILES):
-            grouped_x = turn("x", t, "s")
-            grouped_w1 = turn("w1", t, "v" if t % 2 == 0 else "s")
-            keep_busy(t)
-            quantise("x", t, grouped_x)
-            quantise("w1", t, grouped_w1)
-        for s in range(TILES):
-            if s < HALF:
-                squares(s, s, HALF, "v")
-            squares(s, max(s, HALF), TILES, "s" if s % 2 == 0 else "v")
-            if s > 0:
-                mirror(s, 0, min(s, HALF))
-            if s > HALF:
-                mirror(s, HALF, s)
-            finish(s)
+            SPL = [("x",4),("w1",4),("x",5),("w1",5),("x",6),("w1",6)]
+            bx = turn("x", t, splits.get(("x", t)))
+            bw = turn("w1", t, splits.get(("w1", t)))
+            for nm in ("x", "w1"):
+                if (nm, t + 1) in SPL:
+                    splits[(nm, t + 1)] = split_words("v", nm, t + 1)
+            gx = group("s", bx)
+            gw = group("svsvsvsv"[t], bw)
+            r = {3: 0, 4: 1, 5: 2, 7: 3}.get(t, -1)
+            if r >= 0:
+                early[r] = products(r, 0, r + 1)
+            if t == 7 or r < 0: pass
+            else: copy_h(early[r], "s")
+            quantise("x", t, gx)
+            quantise("w1", t, gw)
+            if 0 <= r and t < 7:
+                multiply(early[r])
+                if r >= 1: square(early[r - 1])
+        square(early[2])
+
+        tasks = [(s, HALF, TILES) for s in range(HALF)] + [(s, s, TILES) for s in range(HALF, TILES)]
+        live = {}
+        def step_products(i):
+            if i < TILES:
+                live[i] = products(*tasks[i])
+        def step_copy(i, e):
+            if i < TILES:
+                copy_h(live[i], e)
+        def step_mult(i, a, b):
+            if i < TILES:
+                multiply(live[i], a, b)
+        mirrors = {}
+        def step_mirror_turn(i):
+            if i < HALF - 1:
+                mirrors[i] = [(i + 1, HALF, mirror_turn(i, i + 1, HALF))]
+            elif HALF <= i < TILES:
+                mirrors[i] = [(0, HALF, mirror_turn(i, 0, HALF))]
+                if i > HALF:
+                    mirrors[i].append((HALF, i, mirror_turn(i, HALF, i)))
+
+        def step_divide(i, part):
+            if 0 <= i < TILES:
+                divide_part(i, part, DIV[i][part])
+        step_products(0)
+        copy_h(early[3], "s")
+        step_copy(0, "s")
+        multiply(early[3])
+        step_products(1)
+        square(early[3])
+        step_mult(0, 0, 1)
+        step_copy(1, "s")
+        for s in range(HALF - 1):
+            step_mirror_turn(s)
+        step_products(2)
+        for i in range(TILES + 1):
+            if i < TILES:
+                square(live[i])
+                for (j0, j1, m) in mirrors.get(i, []):
+                    mirror_copy(i, j0, j1, m, "s")
+            if i + 2 < HALF:
+                step_copy(i + 2, "s")
+            step_products(i + 3)
+            step_mirror_turn(i + 1 if i + 1 >= HALF else TILES)
+            step_mult(i + 1, 0, 1)
+            if i < TILES:
+                total(i)
+            step_divide(i - 1, 0)
+            if i < TILES:
+                invert(i)
+            if i + 2 >= HALF:
+                step_copy(i + 2, "s")
+            step_divide(i - 1, 1)

@@ -64,9 +64,9 @@ def tile_gcn_pa_kernel(tc, x, W1, out):
         for n in range(4):
             nc.tensor.matmul(out=unread[:], lhsT=zeros[:, :P], rhs=zeros[:], start=True, stop=True)
 
-        def keep_busy(t):
+        def keep_busy(t, name="w1"):
             unread = psum.tile([P, BANK], F32, name="bank")
-            nc.tensor.matmul(out=unread[:], lhsT=loaded[("x", t)][:, :P], rhs=loaded[("w1", t)][:, :BANK],
+            nc.tensor.matmul(out=unread[:], lhsT=loaded[("x", t)][:, :P], rhs=loaded[(name, t)][:, :BANK],
                              start=True, stop=True)
 
         def next_part(s):
@@ -215,29 +215,28 @@ def tile_gcn_pa_kernel(tc, x, W1, out):
                 nc.scalar.activation(out=adj[:, c], in_=sq[:, s, c], func=ACT.Copy, scale=totals[s][:, 0:1])
             nc.sync.dma_start(out=out[s * P:(s + 1) * P, c], in_=adj[:, c])
 
-        DIV = ["vv","vv","vv","vv","vv","vv","vv","vs"]
+        DIV = ["V-"]*7+["vs"]
         early = {}
-        splits = {}
+        waiting = []
         for t in range(TILES):
-            SPL = [("x",4),("w1",4),("x",5),("w1",5),("x",6),("w1",6)]
-            bx = turn("x", t, splits.get(("x", t)))
-            bw = turn("w1", t, splits.get(("w1", t)))
-            for nm in ("x", "w1"):
-                if (nm, t + 1) in SPL:
-                    splits[(nm, t + 1)] = split_words("v", nm, t + 1)
+            bx = turn("x", t)
+            if t in (0,):
+                keep_busy(t, "x")
+            bw = turn("w1", t)
+            if t in (0,1,2,3):
+                keep_busy(t)
             gx = group("s", bx)
             gw = group("svsvsvsv"[t], bw)
-            r = {3: 0, 4: 1, 5: 2, 7: 3}.get(t, -1)
-            if r >= 0:
-                early[r] = products(r, 0, r + 1)
-            if t == 7 or r < 0: pass
-            else: copy_h(early[r], "s")
             quantise("x", t, gx)
             quantise("w1", t, gw)
-            if 0 <= r and t < 7:
+            for r in {4:[0],5:[1],7:[2,3]}.get(t, []):
+                early[r] = products(r, 0, r + 1)
+            for r in {4:[0],5:[1],7:[2,3]}.get(t, []):
+                copy_h(early[r], "ssss"[r])
                 multiply(early[r])
-                if r >= 1: square(early[r - 1])
-        square(early[2])
+                for w in waiting:
+                    square(early[w])
+                waiting = [r]
 
         tasks = [(s, HALF, TILES) for s in range(HALF)] + [(s, s, TILES) for s in range(HALF, TILES)]
         live = {}
@@ -263,31 +262,35 @@ def tile_gcn_pa_kernel(tc, x, W1, out):
             if 0 <= i < TILES:
                 divide_part(i, part, DIV[i][part])
         step_products(0)
-        copy_h(early[3], "s")
-        step_copy(0, "s")
-        multiply(early[3])
+        step_copy(0, "ssssssss"[0])
+        for w in waiting:
+            square(early[w])
         step_products(1)
-        square(early[3])
+        step_copy(1, "ssssssss"[1])
         step_mult(0, 0, 1)
-        step_copy(1, "s")
         for s in range(HALF - 1):
             step_mirror_turn(s)
         step_products(2)
         for i in range(TILES + 1):
             if i < TILES:
-                square(live[i])
-                for (j0, j1, m) in mirrors.get(i, []):
+                for (j0, j1, m) in (mirrors.get(i, []) if i < HALF else []):
                     mirror_copy(i, j0, j1, m, "s")
-            if i + 2 < HALF:
-                step_copy(i + 2, "s")
+                square(live[i])
+                for (j0, j1, m) in (mirrors.get(i, []) if i >= HALF else []):
+                    mirror_copy(i, j0, j1, m, "v" if j0 in () else "s")
+            if i + 2 < TILES:
+                step_copy(i + 2, "ssssssss"[i + 2])
             step_products(i + 3)
             step_mirror_turn(i + 1 if i + 1 >= HALF else TILES)
             step_mult(i + 1, 0, 1)
             if i < TILES:
                 total(i)
-            step_divide(i - 1, 0)
+            if i >= 1 and DIV[i-1][0] == "V":
+                step_divide(i - 1, 0)
             if i < TILES:
                 invert(i)
-            if i + 2 >= HALF:
-                step_copy(i + 2, "s")
-            step_divide(i - 1, 1)
+                if DIV[i][0] == "G":
+                    step_divide(i, 0)
+            if i >= 1 and DIV[i-1][0] not in "VG":
+                step_divide(i - 1, 0)
+                step_divide(i - 1, 1)

@@ -215,7 +215,7 @@ def tile_gcn_pa_kernel(tc, x, W1, out):
                 nc.scalar.activation(out=adj[:, c], in_=sq[:, s, c], func=ACT.Copy, scale=totals[s][:, 0:1])
             nc.sync.dma_start(out=out[s * P:(s + 1) * P, c], in_=adj[:, c])
 
-        DIV = ["V-"]*7+["vs"]
+        DIV = ["G-"]*4+["V-"]*3+["vs"]
         early = {}
         waiting = []
         for t in range(TILES):
@@ -223,15 +223,15 @@ def tile_gcn_pa_kernel(tc, x, W1, out):
             if t in (0,):
                 keep_busy(t, "x")
             bw = turn("w1", t)
-            if t in (0,1,2,3):
+            if t in (0,1,2):
                 keep_busy(t)
             gx = group("s", bx)
-            gw = group("svsvsvsv"[t], bw)
+            gw = group("svsvsvss"[t], bw)
             quantise("x", t, gx)
             quantise("w1", t, gw)
-            for r in {4:[0],5:[1],7:[2,3]}.get(t, []):
+            for r in {3:[0],5:[1],7:[2,3]}.get(t, []):
                 early[r] = products(r, 0, r + 1)
-            for r in {4:[0],5:[1],7:[2,3]}.get(t, []):
+            for r in {3:[0],5:[1],7:[2,3]}.get(t, []):
                 copy_h(early[r], "ssss"[r])
                 multiply(early[r])
                 for w in waiting:
@@ -274,20 +274,21 @@ def tile_gcn_pa_kernel(tc, x, W1, out):
         for i in range(TILES + 1):
             if i < TILES:
                 for (j0, j1, m) in (mirrors.get(i, []) if i < HALF else []):
-                    mirror_copy(i, j0, j1, m, "s")
+                    mirror_copy(i, j0, j1, m, "v")
                 square(live[i])
                 for (j0, j1, m) in (mirrors.get(i, []) if i >= HALF else []):
-                    mirror_copy(i, j0, j1, m, "v" if j0 in () else "s")
-            if i + 2 < TILES:
-                step_copy(i + 2, "ssssssss"[i + 2])
+                    mirror_copy(i, j0, j1, m, "v" if (i, j0) in ((4, 0), (5, 4)) else "s")
+            if i + 2 < TILES and "ssssssss"[i + 2] == "s":
+                step_copy(i + 2, "s")
             step_products(i + 3)
             step_mirror_turn(i + 1 if i + 1 >= HALF else TILES)
             step_mult(i + 1, 0, 1)
-            if i < TILES:
-                total(i)
             if i >= 1 and DIV[i-1][0] == "V":
                 step_divide(i - 1, 0)
+            if i + 2 < TILES and "ssssssss"[i + 2] == "v":
+                step_copy(i + 2, "v")
             if i < TILES:
+                total(i)
                 invert(i)
                 if DIV[i][0] == "G":
                     step_divide(i, 0)

@@ -17,12 +17,17 @@ N = 1024
 D = 1024
 WORD = 4
 PASSES = D // (P * WORD)
-WORD_BLOCKS = D // 2 // P
+WORD_SQUARES = D // 2 // P
 TILES = N // P
 HALF = TILES // 2
 BANK = HALF * P
 PARTS = 4
 FLOPS = 2 * N * N * D
+
+EARLY_ROWS = {3: (0,), 5: (1,), TILES - 1: (2, 3)}
+VECTOR_COPIES_W1 = (1, 3, 5, 6)
+VECTOR_COPIES_H = (0, 6)
+GPSIMD_DIVIDES = (0, 1, 2, 3)
 
 
 def tile_gcn_pa_kernel(tc, x, W1, out):
@@ -64,7 +69,7 @@ def tile_gcn_pa_kernel(tc, x, W1, out):
         for n in range(4):
             nc.tensor.matmul(out=unread[:], lhsT=zeros[:, :P], rhs=zeros[:], start=True, stop=True)
 
-        def keep_busy(t, name="w1"):
+        def keep_busy(name, t):
             unread = psum.tile([P, BANK], F32, name="bank")
             nc.tensor.matmul(out=unread[:], lhsT=loaded[("x", t)][:, :P], rhs=loaded[(name, t)][:, :BANK],
                              start=True, stop=True)
@@ -74,37 +79,24 @@ def tile_gcn_pa_kernel(tc, x, W1, out):
             parts_used[s] = c + 1
             return row_sums[:, s, c:c + 1]
 
-        def copy_out(engine, dst, src):
-            if engine == "v":
+        def copy_out(on_vector, dst, src):
+            if on_vector:
                 nc.vector.tensor_copy(out=dst, in_=src)
             else:
                 nc.scalar.copy(out=dst, in_=src)
 
-        def split_words(engine, name, t):
-            split = grp.tile([P, BANK], F32, name="split")
-            dst = split[:].rearrange("p (g u i) -> p g u i", g=PASSES, u=2)
-            src = loaded[(name, t)][:].bitcast(F32).rearrange("p (g i u) -> p g u i", g=PASSES, u=2)
-            if engine == "v":
-                nc.vector.tensor_copy(out=dst, in_=src)
-            elif engine == "s":
-                nc.scalar.copy(out=dst, in_=src)
-            else:
-                nc.gpsimd.tensor_copy(out=dst, in_=src)
-            return split
-
-        def turn(name, t, split=None):
+        def turn(name, t):
             words = loaded[(name, t)][:].bitcast(F32)
             turned = psum.tile([P, BANK], F32, name="bank")
-            for q in range(WORD_BLOCKS):
+            for q in range(WORD_SQUARES):
                 g, u = divmod(q, 2)
-                block = (words[:, 2 * P * g + u:2 * P * (g + 1):2] if split is None
-                         else split[:, q * P:(q + 1) * P])
-                nc.tensor.transpose(turned[:, q * P:(q + 1) * P], block, ident[:])
+                nc.tensor.transpose(turned[:, q * P:(q + 1) * P],
+                                    words[:, 2 * P * g + u:2 * P * (g + 1):2], ident[:])
             return turned
 
-        def group(engine, turned):
+        def group(on_vector, turned):
             grouped = grp.tile([P, PASSES * P * WORD], BF16, name="grouped", align_bytes=64)
-            copy_out(engine,
+            copy_out(on_vector,
                      grouped[:].bitcast(F32).rearrange("p (g r u) -> p g r u", g=PASSES, u=2),
                      turned[:].rearrange("p (g u r) -> p g r u", g=PASSES, u=2))
             return grouped
@@ -121,9 +113,9 @@ def tile_gcn_pa_kernel(tc, x, W1, out):
             cuts = []
             j = j0
             while j < j1:
-                blocks = 4 if j1 - j >= 4 else (2 if j1 - j >= 2 else 1)
-                cuts.append((j, j + blocks))
-                j += blocks
+                count = 4 if j1 - j >= 4 else (2 if j1 - j >= 2 else 1)
+                cuts.append((j, j + count))
+                j += count
             return cuts
 
         def product(stationary, moving, s, j0, j1):
@@ -141,157 +133,133 @@ def tile_gcn_pa_kernel(tc, x, W1, out):
                     )
             return bank
 
-        class_of = {}
-
         def products(s, j0, j1):
-            h = product("x", "w1", s, j0, j1)
-            h_t = product("w1", "x", s, j0, j1)
-            return [s, j0, j1, h, h_t]
+            return {"s": s, "j0": j0, "j1": j1, "cols": (j1 - j0) * P,
+                    "h": product("x", "w1", s, j0, j1), "h_t": product("w1", "x", s, j0, j1)}
 
-        def copy_h(p, engine):
-            s, j0, j1, h, h_t = p
-            cols = (j1 - j0) * P
+        def copy_h(stretch, on_vector):
+            cols = stretch["cols"]
             h_sbuf = work.tile([P, BANK], F32, name="h_sbuf")
-            copy_out(engine, h_sbuf[:, :cols], h[:, :cols])
+            copy_out(on_vector, h_sbuf[:, :cols], stretch["h"][:, :cols])
+            stretch["h_sbuf"] = h_sbuf
+
+        def multiply(stretch):
+            cols = stretch["cols"]
             a = work.tile([P, BANK], F32, name="a")
-            p.extend([h_sbuf, a])
+            nc.vector.tensor_tensor(out=a[:, :cols], in0=stretch["h_t"][:, :cols],
+                                    in1=stretch["h_sbuf"][:, :cols], op=ALU.mult)
+            stretch["a"] = a
 
-        def multiply(p, part=0, parts=1):
-            s, j0, j1, h, h_t, h_sbuf, a = p
-            cols = (j1 - j0) * P
-            lo, hi = part * cols // parts, (part + 1) * cols // parts
-            nc.vector.tensor_tensor(out=a[:, lo:hi], in0=h_t[:, lo:hi], in1=h_sbuf[:, lo:hi], op=ALU.mult)
-
-        def square(p):
-            s, j0, j1, h, h_t, h_sbuf, a = p
-            cols = (j1 - j0) * P
-            nc.scalar.activation(out=sq[:, s, j0 * P:j1 * P], in_=a[:, :cols], func=ACT.Square,
+        def square(stretch):
+            s = stretch["s"]
+            nc.scalar.activation(out=sq[:, s, stretch["j0"] * P:stretch["j1"] * P],
+                                 in_=stretch["a"][:, :stretch["cols"]], func=ACT.Square,
                                  accum_out=next_part(s))
 
         def mirror_turn(s, j0, j1):
             bank = psum.tile([P, BANK], F32, name="bank")
             for j in range(j0, j1):
                 nc.tensor.transpose(bank[:, (j - j0) * P:(j - j0 + 1) * P], sq[:, j, s * P:(s + 1) * P], ident[:])
-            return bank
+            return (s, j0, j1, bank)
 
-        def mirror_copy(s, j0, j1, bank, engine="s"):
-            if engine == "v":
-                nc.vector.tensor_scalar(out=sq[:, s, j0 * P:j1 * P], in0=bank[:, :(j1 - j0) * P], scalar1=1.0,
-                                        scalar2=0.0, op0=ALU.mult, op1=ALU.add, accum_out=next_part(s))
-                return
-            nc.scalar.activation(out=sq[:, s, j0 * P:j1 * P], in_=bank[:, :(j1 - j0) * P], func=ACT.Copy,
-                                 accum_out=next_part(s))
+        def mirror_copy(turned, on_vector):
+            s, j0, j1, bank = turned
+            dst = sq[:, s, j0 * P:j1 * P]
+            src = bank[:, :(j1 - j0) * P]
+            if on_vector:
+                nc.vector.tensor_scalar(out=dst, in0=src, scalar1=1.0, scalar2=0.0, op0=ALU.mult, op1=ALU.add,
+                                        accum_out=next_part(s))
+            else:
+                nc.scalar.activation(out=dst, in_=src, func=ACT.Copy, accum_out=next_part(s))
 
         totals = {}
+        inverses = {}
 
-        def total(s):
-            t = small.tile([P, 1], F32, name="total")
-            nc.vector.tensor_reduce(out=t[:], in_=row_sums[:, s, :], axis=AX.X, op=ALU.add)
-            totals[s] = t
+        def add_parts(s):
+            total = small.tile([P, 1], F32, name="total")
+            nc.vector.tensor_reduce(out=total[:], in_=row_sums[:, s, :], axis=AX.X, op=ALU.add)
+            totals[s] = total
 
         def invert(s):
             inverse = small.tile([P, 1], F32, name="inverse")
             nc.vector.reciprocal(out=inverse[:], in_=totals[s][:])
-            totals[s] = inverse
+            inverses[s] = inverse
 
-        adjs = {}
+        def divide(s, engines):
+            adj = rows.tile([P, N], F32, name="adj")
+            width = N // len(engines)
+            for n, engine in enumerate(engines):
+                cols = slice(n * width, (n + 1) * width)
+                factor = inverses[s][:, 0:1]
+                if engine == "vector":
+                    nc.vector.tensor_scalar(out=adj[:, cols], in0=sq[:, s, cols], scalar1=factor, scalar2=None,
+                                            op0=ALU.mult)
+                elif engine == "gpsimd":
+                    nc.gpsimd.tensor_scalar(out=adj[:, cols], in0=sq[:, s, cols], scalar1=factor, scalar2=0.0,
+                                            op0=ALU.mult, op1=ALU.add)
+                else:
+                    nc.scalar.activation(out=adj[:, cols], in_=sq[:, s, cols], func=ACT.Copy, scale=factor)
+                nc.sync.dma_start(out=out[s * P:(s + 1) * P, cols], in_=adj[:, cols])
 
-        def divide_part(s, i, e):
-            if e == "-":
-                return
-            if s not in adjs:
-                adjs[s] = rows.tile([P, N], F32, name="adj")
-            adj = adjs[s]
-            c = slice(i * N // 2, (i + 1) * N // 2)
-            if e in "VG":
-                c = slice(0, N)
-            if e in "vV":
-                nc.vector.tensor_scalar(out=adj[:, c], in0=sq[:, s, c], scalar1=totals[s][:, 0:1], scalar2=None,
-                                        op0=ALU.mult)
-            elif e in "gG":
-                nc.gpsimd.tensor_scalar(out=adj[:, c], in0=sq[:, s, c], scalar1=totals[s][:, 0:1], scalar2=0.0,
-                                        op0=ALU.mult, op1=ALU.add)
-            else:
-                nc.scalar.activation(out=adj[:, c], in_=sq[:, s, c], func=ACT.Copy, scale=totals[s][:, 0:1])
-            nc.sync.dma_start(out=out[s * P:(s + 1) * P, c], in_=adj[:, c])
-
-        DIV = ["G-"]*4+["V-"]*3+["vs"]
-        early = {}
-        waiting = []
+        unsquared = None
         for t in range(TILES):
-            bx = turn("x", t)
-            if t in (0,):
-                keep_busy(t, "x")
-            bw = turn("w1", t)
-            if t in (0,1,2):
-                keep_busy(t)
-            gx = group("s", bx)
-            gw = group("svsvsvss"[t], bw)
-            quantise("x", t, gx)
-            quantise("w1", t, gw)
-            for r in {3:[0],5:[1],7:[2,3]}.get(t, []):
-                early[r] = products(r, 0, r + 1)
-            for r in {3:[0],5:[1],7:[2,3]}.get(t, []):
-                copy_h(early[r], "ssss"[r])
-                multiply(early[r])
-                for w in waiting:
-                    square(early[w])
-                waiting = [r]
+            turned_x = turn("x", t)
+            if t == 0:
+                keep_busy("x", t)
+            turned_w1 = turn("w1", t)
+            if t < min(EARLY_ROWS):
+                keep_busy("w1", t)
+            grouped_x = group(False, turned_x)
+            grouped_w1 = group(t in VECTOR_COPIES_W1, turned_w1)
+            quantise("x", t, grouped_x)
+            quantise("w1", t, grouped_w1)
+            early = [products(s, 0, s + 1) for s in EARLY_ROWS.get(t, ())]
+            for stretch in early:
+                copy_h(stretch, False)
+                multiply(stretch)
+                if unsquared is not None:
+                    square(unsquared)
+                unsquared = stretch
 
-        tasks = [(s, HALF, TILES) for s in range(HALF)] + [(s, s, TILES) for s in range(HALF, TILES)]
         live = {}
-        def step_products(i):
-            if i < TILES:
-                live[i] = products(*tasks[i])
-        def step_copy(i, e):
-            if i < TILES:
-                copy_h(live[i], e)
-        def step_mult(i, a, b):
-            if i < TILES:
-                multiply(live[i], a, b)
         mirrors = {}
-        def step_mirror_turn(i):
-            if i < HALF - 1:
-                mirrors[i] = [(i + 1, HALF, mirror_turn(i, i + 1, HALF))]
-            elif HALF <= i < TILES:
-                mirrors[i] = [(0, HALF, mirror_turn(i, 0, HALF))]
-                if i > HALF:
-                    mirrors[i].append((HALF, i, mirror_turn(i, HALF, i)))
 
-        def step_divide(i, part):
-            if 0 <= i < TILES:
-                divide_part(i, part, DIV[i][part])
-        step_products(0)
-        step_copy(0, "ssssssss"[0])
-        for w in waiting:
-            square(early[w])
-        step_products(1)
-        step_copy(1, "ssssssss"[1])
-        step_mult(0, 0, 1)
+        def start(i):
+            if i < TILES:
+                live[i] = products(i, max(i, HALF), TILES)
+
+        start(0)
+        copy_h(live[0], 0 in VECTOR_COPIES_H)
+        square(unsquared)
+        start(1)
+        copy_h(live[1], 1 in VECTOR_COPIES_H)
+        multiply(live[0])
         for s in range(HALF - 1):
-            step_mirror_turn(s)
-        step_products(2)
-        for i in range(TILES + 1):
-            if i < TILES:
-                for (j0, j1, m) in (mirrors.get(i, []) if i < HALF else []):
-                    mirror_copy(i, j0, j1, m, "v")
-                square(live[i])
-                for (j0, j1, m) in (mirrors.get(i, []) if i >= HALF else []):
-                    mirror_copy(i, j0, j1, m, "v" if (i, j0) in ((4, 0), (5, 4)) else "s")
-            if i + 2 < TILES and "ssssssss"[i + 2] == "s":
-                step_copy(i + 2, "s")
-            step_products(i + 3)
-            step_mirror_turn(i + 1 if i + 1 >= HALF else TILES)
-            step_mult(i + 1, 0, 1)
-            if i >= 1 and DIV[i-1][0] == "V":
-                step_divide(i - 1, 0)
-            if i + 2 < TILES and "ssssssss"[i + 2] == "v":
-                step_copy(i + 2, "v")
-            if i < TILES:
-                total(i)
-                invert(i)
-                if DIV[i][0] == "G":
-                    step_divide(i, 0)
-            if i >= 1 and DIV[i-1][0] not in "VG":
-                step_divide(i - 1, 0)
-                step_divide(i - 1, 1)
+            mirrors[s] = [mirror_turn(s, s + 1, HALF)]
+        start(2)
+        mirror_copy(mirrors[0][0], True)
+        for i in range(TILES):
+            square(live[i])
+            if i >= HALF:
+                for turned in mirrors[i]:
+                    mirror_copy(turned, False)
+            if i + 2 < TILES and i + 2 not in VECTOR_COPIES_H:
+                copy_h(live[i + 2], False)
+            start(i + 3)
+            if HALF <= i + 1 < TILES:
+                mirrors[i + 1] = [mirror_turn(i + 1, 0, HALF)]
+                if i + 1 > HALF:
+                    mirrors[i + 1].append(mirror_turn(i + 1, HALF, i + 1))
+            if i + 1 < TILES:
+                multiply(live[i + 1])
+            if i > 0 and i - 1 not in GPSIMD_DIVIDES:
+                divide(i - 1, ["vector"])
+            if i + 2 in VECTOR_COPIES_H:
+                copy_h(live[i + 2], True)
+            add_parts(i)
+            if i + 1 < HALF - 1:
+                mirror_copy(mirrors[i + 1][0], True)
+            invert(i)
+            if i in GPSIMD_DIVIDES:
+                divide(i, ["gpsimd"])
+        divide(TILES - 1, ["vector", "scalar"])

from contextlib import ExitStack

import concourse.mybir as mybir
from concourse.masks import make_identity

FP8X4 = mybir.dt.float8_e4m3fn_x4
F32 = mybir.dt.float32
BF16 = mybir.dt.bfloat16
U32 = mybir.dt.uint32
U8 = mybir.dt.uint8
ALU = mybir.AluOpType
ACT = mybir.ActivationFunctionType
AX = mybir.AxisListType

P = 128
N = 1024
D = 1024
WORD = 4
PASSES = D // (P * WORD)
WORD_SQUARES = D // 2 // P
TILES = N // P
HALF = TILES // 2
BANK = HALF * P
PARTS = 4
FLOPS = 2 * N * N * D

EARLY_ROWS = {3: (0,), 5: (1,), TILES - 1: (2, 3)}
VECTOR_COPIES_W1 = (1, 3, 5, 6)
VECTOR_COPIES_H = (0, 6)
GPSIMD_DIVIDES = (0, 1, 2, 3)


def tile_gcn_pa_kernel(tc, x, W1, out):
    nc = tc.nc
    with ExitStack() as ctx:
        const = ctx.enter_context(tc.tile_pool(name="const", bufs=1))
        raw = ctx.enter_context(tc.tile_pool(name="raw", bufs=1))
        keep = ctx.enter_context(tc.tile_pool(name="keep", bufs=1))
        grp = ctx.enter_context(tc.tile_pool(name="grp", bufs=6))
        work = ctx.enter_context(tc.tile_pool(name="work", bufs=4))
        rows = ctx.enter_context(tc.tile_pool(name="rows", bufs=4))
        small = ctx.enter_context(tc.tile_pool(name="small", bufs=8))
        psum = ctx.enter_context(tc.psum_pool(name="psum", bufs=8))
        ctx.enter_context(tc.manual_schedule())

        operands = {"x": x, "w1": W1}
        loaded = {}
        for t in range(TILES):
            for name in ("x", "w1"):
                row_tile = raw.tile([P, D], BF16, name="raw_%s_%d" % (name, t))
                nc.sync.dma_start(out=row_tile[:], in_=operands[name][t * P:(t + 1) * P, :])
                loaded[(name, t)] = row_tile

        ident = const.tile([P, P], F32, name="ident")
        make_identity(nc, ident[:])
        zeros = const.tile([P, BANK], BF16, name="zeros")
        nc.vector.memset(zeros[:], 0.0)
        row_sums = const.tile([P, TILES, PARTS], F32, name="row_sums")
        nc.vector.memset(row_sums[:], 0.0)
        parts_used = [0] * TILES
        sq = keep.tile([P, TILES, N], F32, name="sq")
        codes = {}
        scales = {}
        for name in ("x", "w1"):
            codes[name] = keep.tile([P, PASSES, N], U32, name="codes_" + name, align_bytes=64)
            scales[name] = keep.tile([P, PASSES, N], U8, name="scales_" + name, align_bytes=64)

        unread = psum.tile([P, BANK], F32, name="bank")
        for n in range(4):
            nc.tensor.matmul(out=unread[:], lhsT=zeros[:, :P], rhs=zeros[:], start=True, stop=True)

        def keep_busy(name, t):
            unread = psum.tile([P, BANK], F32, name="bank")
            nc.tensor.matmul(out=unread[:], lhsT=loaded[("x", t)][:, :P], rhs=loaded[(name, t)][:, :BANK],
                             start=True, stop=True)

        def next_part(s):
            c = parts_used[s]
            parts_used[s] = c + 1
            return row_sums[:, s, c:c + 1]

        def copy_out(on_vector, dst, src):
            if on_vector:
                nc.vector.tensor_copy(out=dst, in_=src)
            else:
                nc.scalar.copy(out=dst, in_=src)

        def turn(name, t):
            words = loaded[(name, t)][:].bitcast(F32)
            turned = psum.tile([P, BANK], F32, name="bank")
            for q in range(WORD_SQUARES):
                g, u = divmod(q, 2)
                nc.tensor.transpose(turned[:, q * P:(q + 1) * P],
                                    words[:, 2 * P * g + u:2 * P * (g + 1):2], ident[:])
            return turned

        def group(on_vector, turned):
            grouped = grp.tile([P, PASSES * P * WORD], BF16, name="grouped", align_bytes=64)
            copy_out(on_vector,
                     grouped[:].bitcast(F32).rearrange("p (g r u) -> p g r u", g=PASSES, u=2),
                     turned[:].rearrange("p (g u r) -> p g r u", g=PASSES, u=2))
            return grouped

        def quantise(name, t, grouped):
            for g in range(PASSES):
                nc.vector.quantize_mx(
                    out=codes[name][:, g, t * P:(t + 1) * P].bitcast(FP8X4),
                    scales=scales[name][:, g, t * P:(t + 1) * P],
                    in_=grouped[:, g * P * WORD:(g + 1) * P * WORD],
                )

        def moving_cuts(j0, j1):
            cuts = []
            j = j0
            while j < j1:
                count = 4 if j1 - j >= 4 else (2 if j1 - j >= 2 else 1)
                cuts.append((j, j + count))
                j += count
            return cuts

        def product(stationary, moving, s, j0, j1):
            bank = psum.tile([P, BANK], F32, name="bank")
            for (lo, hi) in moving_cuts(j0, j1):
                for g in range(PASSES):
                    nc.tensor.matmul_mx(
                        out=bank[:, (lo - j0) * P:(hi - j0) * P],
                        lhsT=codes[stationary][:, g, s * P:(s + 1) * P].bitcast(FP8X4),
                        lhsT_scale=scales[stationary][:, g, s * P:(s + 1) * P],
                        rhs=codes[moving][:, g, lo * P:hi * P].bitcast(FP8X4),
                        rhs_scale=scales[moving][:, g, lo * P:hi * P],
                        start=(g == 0),
                        stop=(g == PASSES - 1),
                    )
            return bank

        def products(s, j0, j1):
            return {"s": s, "j0": j0, "j1": j1, "cols": (j1 - j0) * P,
                    "h": product("x", "w1", s, j0, j1), "h_t": product("w1", "x", s, j0, j1)}

        def copy_h(stretch, on_vector):
            cols = stretch["cols"]
            h_sbuf = work.tile([P, BANK], F32, name="h_sbuf")
            copy_out(on_vector, h_sbuf[:, :cols], stretch["h"][:, :cols])
            stretch["h_sbuf"] = h_sbuf

        def multiply(stretch):
            cols = stretch["cols"]
            a = work.tile([P, BANK], F32, name="a")
            nc.vector.tensor_tensor(out=a[:, :cols], in0=stretch["h_t"][:, :cols],
                                    in1=stretch["h_sbuf"][:, :cols], op=ALU.mult)
            stretch["a"] = a

        def square(stretch):
            s = stretch["s"]
            nc.scalar.activation(out=sq[:, s, stretch["j0"] * P:stretch["j1"] * P],
                                 in_=stretch["a"][:, :stretch["cols"]], func=ACT.Square,
                                 accum_out=next_part(s))

        def mirror_turn(s, j0, j1):
            bank = psum.tile([P, BANK], F32, name="bank")
            for j in range(j0, j1):
                nc.tensor.transpose(bank[:, (j - j0) * P:(j - j0 + 1) * P], sq[:, j, s * P:(s + 1) * P], ident[:])
            return (s, j0, j1, bank)

        def mirror_copy(turned, on_vector):
            s, j0, j1, bank = turned
            dst = sq[:, s, j0 * P:j1 * P]
            src = bank[:, :(j1 - j0) * P]
            if on_vector:
                nc.vector.tensor_scalar(out=dst, in0=src, scalar1=1.0, scalar2=0.0, op0=ALU.mult, op1=ALU.add,
                                        accum_out=next_part(s))
            else:
                nc.scalar.activation(out=dst, in_=src, func=ACT.Copy, accum_out=next_part(s))

        totals = {}
        inverses = {}

        def add_parts(s):
            total = small.tile([P, 1], F32, name="total")
            nc.vector.tensor_reduce(out=total[:], in_=row_sums[:, s, :], axis=AX.X, op=ALU.add)
            totals[s] = total

        def invert(s):
            inverse = small.tile([P, 1], F32, name="inverse")
            nc.vector.reciprocal(out=inverse[:], in_=totals[s][:])
            inverses[s] = inverse

        def divide(s, engines):
            adj = rows.tile([P, N], F32, name="adj")
            width = N // len(engines)
            for n, engine in enumerate(engines):
                cols = slice(n * width, (n + 1) * width)
                factor = inverses[s][:, 0:1]
                if engine == "vector":
                    nc.vector.tensor_scalar(out=adj[:, cols], in0=sq[:, s, cols], scalar1=factor, scalar2=None,
                                            op0=ALU.mult)
                elif engine == "gpsimd":
                    nc.gpsimd.tensor_scalar(out=adj[:, cols], in0=sq[:, s, cols], scalar1=factor, scalar2=0.0,
                                            op0=ALU.mult, op1=ALU.add)
                else:
                    nc.scalar.activation(out=adj[:, cols], in_=sq[:, s, cols], func=ACT.Copy, scale=factor)
                nc.sync.dma_start(out=out[s * P:(s + 1) * P, cols], in_=adj[:, cols])

        unsquared = None
        for t in range(TILES):
            turned_x = turn("x", t)
            if t == 0:
                keep_busy("x", t)
            turned_w1 = turn("w1", t)
            if t < min(EARLY_ROWS):
                keep_busy("w1", t)
            grouped_x = group(False, turned_x)
            grouped_w1 = group(t in VECTOR_COPIES_W1, turned_w1)
            quantise("x", t, grouped_x)
            quantise("w1", t, grouped_w1)
            early = [products(s, 0, s + 1) for s in EARLY_ROWS.get(t, ())]
            for stretch in early:
                copy_h(stretch, False)
                multiply(stretch)
                if unsquared is not None:
                    square(unsquared)
                unsquared = stretch

        live = {}
        mirrors = {}

        def start(i):
            if i < TILES:
                live[i] = products(i, max(i, HALF), TILES)

        start(0)
        copy_h(live[0], 0 in VECTOR_COPIES_H)
        square(unsquared)
        start(1)
        copy_h(live[1], 1 in VECTOR_COPIES_H)
        multiply(live[0])
        for s in range(HALF - 1):
            mirrors[s] = [mirror_turn(s, s + 1, HALF)]
        start(2)
        mirror_copy(mirrors[0][0], True)
        for i in range(TILES):
            square(live[i])
            if i >= HALF:
                for turned in mirrors[i]:
                    mirror_copy(turned, False)
            if i + 2 < TILES and i + 2 not in VECTOR_COPIES_H:
                copy_h(live[i + 2], False)
            start(i + 3)
            if HALF <= i + 1 < TILES:
                mirrors[i + 1] = [mirror_turn(i + 1, 0, HALF)]
                if i + 1 > HALF:
                    mirrors[i + 1].append(mirror_turn(i + 1, HALF, i + 1))
            if i + 1 < TILES:
                multiply(live[i + 1])
            if i > 0 and i - 1 not in GPSIMD_DIVIDES:
                divide(i - 1, ["vector"])
            if i + 2 in VECTOR_COPIES_H:
                copy_h(live[i + 2], True)
            add_parts(i)
            if i + 1 < HALF - 1:
                mirror_copy(mirrors[i + 1][0], True)
            invert(i)
            if i in GPSIMD_DIVIDES:
                divide(i, ["gpsimd"])
        divide(TILES - 1, ["vector", "scalar"])
